import numpy as np
import ml_dtypes


def mxq(x, axis, fmt="e4m3"):
    dtype, down = {"e4m3": (ml_dtypes.float8_e4m3fn, 7), "e5m2": (ml_dtypes.float8_e5m2, 14)}[fmt]
    v = np.moveaxis(np.asarray(x, np.float32).astype(ml_dtypes.bfloat16).astype(np.float64), axis, -1)
    blocks = v.reshape(v.shape[:-1] + (-1, 32))
    amax = np.abs(blocks).max(-1, keepdims=True)
    byte = np.maximum(np.where(amax > 0, np.frexp(amax)[1] - 1 + 127, 0) - down, 1)
    scale = np.exp2(byte - 127.0)
    codes = (blocks / scale).astype(np.float32).astype(dtype).astype(np.float64)
    return np.moveaxis((codes * scale).reshape(v.shape), -1, axis)


WIDE = False


def mx_kscale(k):
    if not WIDE:
        return np.ones(k)
    levels = np.array([30, -30])
    if k % 512:
        return np.exp2(np.random.permutation(np.resize(levels, k // 32))).repeat(32)
    a = np.empty((k // 512, 16))
    for p in range(k // 512):
        a[p, :8] = np.random.permutation(np.resize(levels, 8))
        for g in range(8):
            far = levels[np.abs(levels - a[p, g]) >= 10]
            a[p, g + 8] = far[np.random.randint(len(far))]
    return np.exp2(a.ravel()).repeat(32)


BF16 = ml_dtypes.bfloat16


def bf(x):
    return np.asarray(x, np.float32).astype(BF16)


def f64(x):
    return np.asarray(x).astype(np.float64)


B, C, P, Q, R = 1024, 1024, 16, 16, 16
D = P * Q * R


def setup_inputs():
    s = mx_kscale(D).reshape(P, Q, R)
    return {"core": bf(np.random.standard_normal((B, P, Q, R)) * s),
            "weights": bf(np.random.standard_normal((C, P, Q, R)) / np.sqrt(D) / s)}


def reference(core, weights):
    b = core.shape[0]
    c = weights.shape[0]
    x = mxq(f64(core).reshape(b, -1), 1, "e5m2")
    w = mxq(f64(weights).reshape(c, -1), 1, "e4m3")
    return x @ w.T

@@ -1,0 +1,200 @@
+from contextlib import ExitStack
+
+import concourse.mybir as mybir
+from concourse.masks import make_identity
+
+ROWS = 1024
+K = 4096
+FLOPS = 2 * ROWS * ROWS * K
+
+F32 = mybir.dt.float32
+BF16 = mybir.dt.bfloat16
+U32 = mybir.dt.uint32
+U8 = mybir.dt.uint8
+E5X4 = mybir.dt.float8_e5m2_x4
+E4X4 = mybir.dt.float8_e4m3fn_x4
+
+P = 128
+KP = 512
+NPASS = K // KP
+NU = 32
+PERM_AHEAD = 3
+RAW_BUFS = 10
+
+
+def tile_tensoroutputlayer_kernel(tc, core, weights, out):
+    nc = tc.nc
+    x2d = core.rearrange("b i j k -> b (i j k)")
+    w2d = weights.rearrange("c i j k -> c (i j k)")
+
+    with ExitStack() as ctx:
+        const = ctx.enter_context(tc.tile_pool(name="const", bufs=1))
+        keep = ctx.enter_context(tc.tile_pool(name="keep", bufs=1))
+        rawp = ctx.enter_context(tc.tile_pool(name="rawp", bufs=RAW_BUFS))
+        permp = ctx.enter_context(tc.tile_pool(name="permp", bufs=4))
+        grpp = ctx.enter_context(tc.tile_pool(name="grpp", bufs=4))
+        outp = ctx.enter_context(tc.tile_pool(name="outp", bufs=4))
+        trp = ctx.enter_context(tc.psum_pool(name="trp", bufs=4))
+        accp = ctx.enter_context(tc.psum_pool(name="accp", bufs=4))
+
+        ident = const.tile([P, P], F32, name="ident")
+        make_identity(nc, ident[:])
+        warm = const.tile([P, 8], F32, name="warm")
+        nc.scalar.copy(out=warm[:, 0:1], in_=ident[:, 0:1])
+
+        loads = []
+        unit_src = {}
+        for c in (0, 1):
+            unit_src[2 * c] = (len(loads), 0)
+            loads.append((w2d, 0, 4, c * KP, KP))
+            unit_src[2 * c + 1] = (len(loads), 0)
+            loads.append((x2d, 0, 4, c * KP, KP))
+        for c in (2, 4, 6):
+            unit_src[2 * c] = (len(loads), 0)
+            unit_src[2 * c + 2] = (len(loads), 1)
+            loads.append((w2d, 0, 4, c * KP, 2 * KP))
+            unit_src[2 * c + 1] = (len(loads), 0)
+            unit_src[2 * c + 3] = (len(loads), 1)
+            loads.append((x2d, 0, 4, c * KP, 2 * KP))
+        for c in (0, 2, 4, 6):
+            unit_src[16 + c] = (len(loads), 0)
+            unit_src[16 + c + 1] = (len(loads), 1)
+            loads.append((w2d, 512, 4, c * KP, 2 * KP))
+        for m in range(4):
+            unit_src[24 + 2 * m] = (len(loads), 0)
+            unit_src[24 + 2 * m + 1] = (len(loads), 1)
+            loads.append((x2d, 512 + m * P, 1, 0, K))
+        last_user = {}
+        for j in range(NU):
+            last_user[unit_src[j][0]] = j
+
+        raw_tiles = {}
+        state = {"next_load": 0}
+
+        def issue_load():
+            i = state["next_load"]
+            if i >= len(loads):
+                return
+            state["next_load"] = i + 1
+            src, r0, nt, k0, kw = loads[i]
+            raw = rawp.tile([P, nt, kw], BF16, name="raw", tag="raw")
+            nc.sync.dma_start(
+                out=raw[:],
+                in_=src[r0 : r0 + nt * P, k0 : k0 + kw].rearrange("(a p) k -> p a k", p=P),
+            )
+            raw_tiles[i] = raw
+
+        perm_tiles = {}
+        bank_tiles = {}
+        grp_tiles = {}
+        codes = {}
+        scales = {}
+
+        def permute(j):
+            li, piece = unit_src[j]
+            raw = raw_tiles[li]
+            perm = permp.tile([P, 4, 2, P], F32, name="perm", tag="perm")
+            if j < 24:
+                words = raw[:, :, piece * KP : (piece + 1) * KP].bitcast(F32)
+                src = words.rearrange("p a (q u) -> p a u q", u=2)
+            else:
+                words = raw[:, 0, piece * 4 * KP : (piece + 1) * 4 * KP].bitcast(F32)
+                src = words.rearrange("p (a q u) -> p a u q", a=4, u=2)
+            nc.vector.tensor_copy(out=perm[:], in_=src)
+            perm_tiles[j] = perm
+            if last_user[li] == j:
+                issue_load()
+
+        def transposes(j):
+            perm = perm_tiles[j]
+            banks = []
+            for b in range(2):
+                bank = trp.tile([P, 2, 2, P], F32, name="trb", tag="trb")
+                for a in range(2):
+                    for u in range(2):
+                        nc.tensor.transpose(bank[:, a, u, :], perm[:, 2 * b + a, u, :], ident[:])
+                banks.append(bank)
+            bank_tiles[j] = banks
+
+        def evacuate(j):
+            grp = grpp.tile([P, 4 * P, 4], BF16, name="grp", tag="grp", align_bytes=64)
+            gw = grp[:].bitcast(F32)
+            for b in range(2):
+                nc.scalar.copy(
+                    out=gw[:, 2 * P * b : 2 * P * (b + 1), :].rearrange("p (a r) u -> p a r u", a=2),
+                    in_=bank_tiles[j][b][:].rearrange("p a u r -> p a r u"),
+                )
+            grp_tiles[j] = grp
+
+        def is_x(j):
+            return j >= 24 or (j < 16 and j % 2 == 1)
+
+        def quantize(j):
+            cd = keep.tile([P, 4 * P], U32, name="cd%d" % j, tag="cd%d" % j, align_bytes=64)
+            sc = keep.tile([P, 4 * P], U8, name="sc%d" % j, tag="sc%d" % j, align_bytes=64)
+            nc.vector.quantize_mx(
+                out=cd[:].bitcast(E5X4 if is_x(j) else E4X4),
+                scales=sc[:],
+                in_=grp_tiles[j][:].rearrange("p w t -> p (w t)"),
+            )
+            codes[j] = cd
+            scales[j] = sc
+
+        def w_unit(h, c):
+            return 2 * c if h == 0 else 16 + c
+
+        def mx(acc, xj, xcol, h, c):
+            wj = w_unit(h, c)
+            nc.tensor.matmul_mx(
+                out=acc[:],
+                lhsT=codes[xj][:, xcol * P : (xcol + 1) * P].bitcast(E5X4),
+                lhsT_scale=scales[xj][:, xcol * P : (xcol + 1) * P],
+                rhs=codes[wj][:].bitcast(E4X4),
+                rhs_scale=scales[wj][:],
+                start=(c == 0),
+                stop=(c == NPASS - 1),
+            )
+
+        def store(acc, m, h, on_vector):
+            osb = outp.tile([P, 4 * P], F32, name="osb", tag="osb")
+            if on_vector:
+                nc.vector.tensor_copy(out=osb[:], in_=acc[:])
+            else:
+                nc.scalar.copy(out=osb[:], in_=acc[:])
+            nc.sync.dma_start(out=out[m * P : (m + 1) * P, h * 512 : (h + 1) * 512], in_=osb[:])
+
+        accs = {}
+
+        def multiply(r):
+            if r < 12:
+                h = 0 if r < 8 else 1
+                passes = [r] if r < 8 else [2 * (r - 8), 2 * (r - 8) + 1]
+                for c in passes:
+                    for m in range(4):
+                        if c == 0:
+                            accs[m] = accp.tile([P, 4 * P], F32, name="acc", tag="acc")
+                        mx(accs[m], 2 * c + 1, m, h, c)
+                if passes[-1] == NPASS - 1:
+                    for m in range(4):
+                        store(accs[m], m, h, m % 2 == 0)
+            else:
+                m = r - 12
+                for h in range(2):
+                    acc = accp.tile([P, 4 * P], F32, name="acc", tag="acc")
+                    for c in range(NPASS):
+                        mx(acc, 24 + 2 * m + c // 4, c % 4, h, c)
+                    store(acc, 4 + m, h, h == 0)
+
+        with tc.manual_schedule():
+            for i in range(RAW_BUFS):
+                issue_load()
+            for k in range(-PERM_AHEAD, NU + 1):
+                if 0 <= k + PERM_AHEAD < NU:
+                    permute(k + PERM_AHEAD)
+                if 0 <= k + 1 < NU:
+                    transposes(k + 1)
+                    evacuate(k + 1)
+                if 0 <= k < NU:
+                    quantize(k)
+                if k >= 2 and k % 2 == 0:
+                    multiply((k - 2) // 2)

@@ -17,9 +17,18 @@ E4X4 = mybir.dt.float8_e4m3fn_x4
 P = 128
 KP = 512
 NPASS = K // KP
-NU = 32
 PERM_AHEAD = 3
-RAW_BUFS = 10
+RAW_BUFS = 9
+ACC_BANKS = 4
+
+ITEMS = (
+    [("W", 0, 0), ("W", 0, 2), ("X", 0), ("X", 1), ("X", 2), ("X", 3), ("W", 0, 4), ("W", 0, 6)]
+    + [("W", 1, c) for c in (0, 2, 4, 6)]
+    + [("X", 4), ("X", 5), ("V", 6), ("V", 7)]
+)
+GROUPS = [(m, 0) for m in range(4)] + [(m, 1) for m in range(4)] + [(m, h) for m in range(4, 8) for h in range(2)]
+V_FIRST_TICK = 20
+V_TICK_STEP = 3
 
 
 def tile_tensoroutputlayer_kernel(tc, core, weights, out):
@@ -31,78 +40,80 @@ def tile_tensoroutputlayer_kernel(tc, core, weights, out):
         const = ctx.enter_context(tc.tile_pool(name="const", bufs=1))
         keep = ctx.enter_context(tc.tile_pool(name="keep", bufs=1))
         rawp = ctx.enter_context(tc.tile_pool(name="rawp", bufs=RAW_BUFS))
-        permp = ctx.enter_context(tc.tile_pool(name="permp", bufs=4))
-        grpp = ctx.enter_context(tc.tile_pool(name="grpp", bufs=4))
+        permp = ctx.enter_context(tc.tile_pool(name="permp", bufs=5))
+        grpp = ctx.enter_context(tc.tile_pool(name="grpp", bufs=5))
+        vecp = ctx.enter_context(tc.tile_pool(name="vecp", bufs=2))
         outp = ctx.enter_context(tc.tile_pool(name="outp", bufs=4))
         trp = ctx.enter_context(tc.psum_pool(name="trp", bufs=4))
-        accp = ctx.enter_context(tc.psum_pool(name="accp", bufs=4))
+        accp = ctx.enter_context(tc.psum_pool(name="accp", bufs=ACC_BANKS))
 
         ident = const.tile([P, P], F32, name="ident")
         make_identity(nc, ident[:])
         warm = const.tile([P, 8], F32, name="warm")
         nc.scalar.copy(out=warm[:, 0:1], in_=ident[:, 0:1])
 
-        loads = []
-        unit_src = {}
-        for c in (0, 1):
-            unit_src[2 * c] = (len(loads), 0)
-            loads.append((w2d, 0, 4, c * KP, KP))
-            unit_src[2 * c + 1] = (len(loads), 0)
-            loads.append((x2d, 0, 4, c * KP, KP))
-        for c in (2, 4, 6):
-            unit_src[2 * c] = (len(loads), 0)
-            unit_src[2 * c + 2] = (len(loads), 1)
-            loads.append((w2d, 0, 4, c * KP, 2 * KP))
-            unit_src[2 * c + 1] = (len(loads), 0)
-            unit_src[2 * c + 3] = (len(loads), 1)
-            loads.append((x2d, 0, 4, c * KP, 2 * KP))
-        for c in (0, 2, 4, 6):
-            unit_src[16 + c] = (len(loads), 0)
-            unit_src[16 + c + 1] = (len(loads), 1)
-            loads.append((w2d, 512, 4, c * KP, 2 * KP))
-        for m in range(4):
-            unit_src[24 + 2 * m] = (len(loads), 0)
-            unit_src[24 + 2 * m + 1] = (len(loads), 1)
-            loads.append((x2d, 512 + m * P, 1, 0, K))
-        last_user = {}
-        for j in range(NU):
-            last_user[unit_src[j][0]] = j
+        units = []
+        vunits = []
+        for i, it in enumerate(ITEMS):
+            for piece in range(2):
+                if it[0] == "W":
+                    units.append(("W", it[1], it[2] + piece, i, piece))
+                elif it[0] == "X":
+                    units.append(("X", it[1], piece, i, piece))
+                else:
+                    vunits.append(("X", it[1], piece, i, piece))
+        nu = len(units)
 
         raw_tiles = {}
-        state = {"next_load": 0}
+        state = {"next_load": 0, "next_perm": 0, "open": 0, "stores": 0}
 
         def issue_load():
             i = state["next_load"]
-            if i >= len(loads):
+            if i >= len(ITEMS):
                 return
             state["next_load"] = i + 1
-            src, r0, nt, k0, kw = loads[i]
-            raw = rawp.tile([P, nt, kw], BF16, name="raw", tag="raw")
-            nc.sync.dma_start(
-                out=raw[:],
-                in_=src[r0 : r0 + nt * P, k0 : k0 + kw].rearrange("(a p) k -> p a k", p=P),
-            )
+            it = ITEMS[i]
+            if it[0] == "W":
+                raw = rawp.tile([P, 4, 2 * KP], BF16, name="raw", tag="raw")
+                r0 = it[1] * 512
+                k0 = it[2] * KP
+                nc.sync.dma_start(
+                    out=raw[:],
+                    in_=w2d[r0 : r0 + 512, k0 : k0 + 2 * KP].rearrange("(a p) k -> p a k", p=P),
+                )
+            elif it[0] == "X":
+                raw = rawp.tile([P, K], BF16, name="raw", tag="raw")
+                nc.sync.dma_start(out=raw[:], in_=x2d[it[1] * P : (it[1] + 1) * P, :])
+            else:
+                raw = rawp.tile([P, NPASS, 4, P], BF16, name="raw", tag="raw")
+                for a in range(4):
+                    for q in range(4):
+                        r0 = it[1] * P + 32 * q
+                        nc.sync.dma_start(
+                            out=raw[32 * a : 32 * a + 32, :, q, :],
+                            in_=x2d[r0 : r0 + 32, :].rearrange("i (c a k) -> i c a k", a=4, k=P)[:, :, a, :],
+                        )
             raw_tiles[i] = raw
 
         perm_tiles = {}
         bank_tiles = {}
         grp_tiles = {}
         codes = {}
-        scales = {}
+        ready = {}
 
         def permute(j):
-            li, piece = unit_src[j]
-            raw = raw_tiles[li]
+            kind, a0, b0, item, piece = units[j]
+            raw = raw_tiles[item]
             perm = permp.tile([P, 4, 2, P], F32, name="perm", tag="perm")
-            if j < 24:
+            if kind == "W":
                 words = raw[:, :, piece * KP : (piece + 1) * KP].bitcast(F32)
                 src = words.rearrange("p a (q u) -> p a u q", u=2)
             else:
-                words = raw[:, 0, piece * 4 * KP : (piece + 1) * 4 * KP].bitcast(F32)
+                words = raw[:, piece * 4 * KP : (piece + 1) * 4 * KP].bitcast(F32)
                 src = words.rearrange("p (a q u) -> p a u q", a=4, u=2)
             nc.vector.tensor_copy(out=perm[:], in_=src)
             perm_tiles[j] = perm
-            if last_user[li] == j:
+            if piece == 1:
                 issue_load()
 
         def transposes(j):
@@ -124,77 +135,113 @@ def tile_tensoroutputlayer_kernel(tc, core, weights, out):
                     out=gw[:, 2 * P * b : 2 * P * (b + 1), :].rearrange("p (a r) u -> p a r u", a=2),
                     in_=bank_tiles[j][b][:].rearrange("p a u r -> p a r u"),
                 )
-            grp_tiles[j] = grp
+            grp_tiles[units[j][0:3]] = grp
 
-        def is_x(j):
-            return j >= 24 or (j < 16 and j % 2 == 1)
-
-        def quantize(j):
-            cd = keep.tile([P, 4 * P], U32, name="cd%d" % j, tag="cd%d" % j, align_bytes=64)
-            sc = keep.tile([P, 4 * P], U8, name="sc%d" % j, tag="sc%d" % j, align_bytes=64)
+        def quantize(key, tick):
+            nm = "%s%d%d" % key
+            cd = keep.tile([P, 4 * P], U32, name="cd" + nm, tag="cd" + nm, align_bytes=64)
+            sc = keep.tile([P, 4 * P], U8, name="sc" + nm, tag="sc" + nm, align_bytes=64)
             nc.vector.quantize_mx(
-                out=cd[:].bitcast(E5X4 if is_x(j) else E4X4),
+                out=cd[:].bitcast(E5X4 if key[0] == "X" else E4X4),
                 scales=sc[:],
-                in_=grp_tiles[j][:].rearrange("p w t -> p (w t)"),
+                in_=grp_tiles[key][:].rearrange("p w t -> p (w t)"),
             )
-            codes[j] = cd
-            scales[j] = sc
+            codes[key] = (cd, sc)
+            ready[key] = tick
 
-        def w_unit(h, c):
-            return 2 * c if h == 0 else 16 + c
+        vperm = {}
+        vturn = {}
 
-        def mx(acc, xj, xcol, h, c):
-            wj = w_unit(h, c)
-            nc.tensor.matmul_mx(
-                out=acc[:],
-                lhsT=codes[xj][:, xcol * P : (xcol + 1) * P].bitcast(E5X4),
-                lhsT_scale=scales[xj][:, xcol * P : (xcol + 1) * P],
-                rhs=codes[wj][:].bitcast(E4X4),
-                rhs_scale=scales[wj][:],
-                start=(c == 0),
-                stop=(c == NPASS - 1),
+        def v_permute(i):
+            kind, m, g, item, piece = vunits[i]
+            raw = raw_tiles[item]
+            t = vecp.tile([P, 16, 2, 32], F32, name="vperm", tag="vperm", align_bytes=64)
+            words = raw[:, 4 * g : 4 * g + 4, :, :].rearrange("p c q k -> p (c q k)").bitcast(F32)
+            nc.scalar.copy(out=t[:], in_=words.rearrange("p (b j u) -> p b u j", j=32, u=2))
+            vperm[i] = t
+            if piece == 1:
+                issue_load()
+
+        def v_transpose(i):
+            t = vecp.tile([P, 1024], F32, name="vturn", tag="vturn", align_bytes=64)
+            nc.vector.transpose(out=t[:], in_=vperm[i][:].rearrange("p b u j -> p (b u j)"))
+            vturn[i] = t
+
+        def v_interleave(i):
+            grp = grpp.tile([P, 4 * P, 4], BF16, name="grp", tag="grp", align_bytes=64)
+            nc.vector.tensor_copy(
+                out=grp[:].bitcast(F32).rearrange("p (b i) u -> p b i u", i=32),
+                in_=vturn[i][:].rearrange("p (b u i) -> p b i u", u=2, i=32),
             )
+            grp_tiles[vunits[i][0:3]] = grp
 
-        def store(acc, m, h, on_vector):
+        def store(acc, m, h):
+            n = state["stores"]
+            state["stores"] = n + 1
             osb = outp.tile([P, 4 * P], F32, name="osb", tag="osb")
-            if on_vector:
-                nc.vector.tensor_copy(out=osb[:], in_=acc[:])
-            else:
-                nc.scalar.copy(out=osb[:], in_=acc[:])
+            nc.scalar.copy(out=osb[:], in_=acc[:])
             nc.sync.dma_start(out=out[m * P : (m + 1) * P, h * 512 : (h + 1) * 512], in_=osb[:])
 
+        done = {}
         accs = {}
 
-        def multiply(r):
-            if r < 12:
-                h = 0 if r < 8 else 1
-                passes = [r] if r < 8 else [2 * (r - 8), 2 * (r - 8) + 1]
-                for c in passes:
-                    for m in range(4):
-                        if c == 0:
-                            accs[m] = accp.tile([P, 4 * P], F32, name="acc", tag="acc")
-                        mx(accs[m], 2 * c + 1, m, h, c)
-                if passes[-1] == NPASS - 1:
-                    for m in range(4):
-                        store(accs[m], m, h, m % 2 == 0)
-            else:
-                m = r - 12
-                for h in range(2):
-                    acc = accp.tile([P, 4 * P], F32, name="acc", tag="acc")
-                    for c in range(NPASS):
-                        mx(acc, 24 + 2 * m + c // 4, c % 4, h, c)
-                    store(acc, 4 + m, h, h == 0)
+        def multiply(tick):
+            for grp_key in GROUPS:
+                m, h = grp_key
+                d = done.setdefault(grp_key, [])
+                if len(d) == NPASS:
+                    continue
+                avail = [
+                    c
+                    for c in range(NPASS)
+                    if c not in d
+                    and ready.get(("X", m, c // 4), tick) < tick
+                    and ready.get(("W", h, c), tick) < tick
+                ]
+                if grp_key not in accs:
+                    if len(avail) == 0 or state["open"] >= ACC_BANKS:
+                        return
+                    accs[grp_key] = accp.tile([P, 4 * P], F32, name="acc", tag="acc")
+                    state["open"] = state["open"] + 1
+                for c in avail:
+                    xc, xs = codes[("X", m, c // 4)]
+                    wc, ws = codes[("W", h, c)]
+                    col = (c % 4) * P
+                    nc.tensor.matmul_mx(
+                        out=accs[grp_key][:],
+                        lhsT=xc[:, col : col + P].bitcast(E5X4),
+                        lhsT_scale=xs[:, col : col + P],
+                        rhs=wc[:].bitcast(E4X4),
+                        rhs_scale=ws[:],
+                        start=(len(d) == 0),
+                        stop=(len(d) == NPASS - 1),
+                    )
+                    d.append(c)
+                if len(d) == NPASS:
+                    store(accs[grp_key], m, h)
+                    state["open"] = state["open"] - 1
 
         with tc.manual_schedule():
             for i in range(RAW_BUFS):
                 issue_load()
-            for k in range(-PERM_AHEAD, NU + 1):
-                if 0 <= k + PERM_AHEAD < NU:
-                    permute(k + PERM_AHEAD)
-                if 0 <= k + 1 < NU:
-                    transposes(k + 1)
-                    evacuate(k + 1)
-                if 0 <= k < NU:
-                    quantize(k)
-                if k >= 2 and k % 2 == 0:
-                    multiply((k - 2) // 2)
+            for tick in range(-PERM_AHEAD, nu + 12):
+                for j in range(state["next_perm"], min(nu, tick + PERM_AHEAD + 1)):
+                    permute(j)
+                    state["next_perm"] = j + 1
+                if 0 <= tick + 1 < nu:
+                    transposes(tick + 1)
+                    evacuate(tick + 1)
+                if 0 <= tick < nu:
+                    quantize(units[tick][0:3], tick)
+                if tick >= V_FIRST_TICK and (tick - V_FIRST_TICK) % V_TICK_STEP == 0:
+                    s = (tick - V_FIRST_TICK) // V_TICK_STEP
+                    if 0 <= s - 3 < len(vunits):
+                        quantize(vunits[s - 3][0:3], tick)
+                    if 0 <= s - 2 < len(vunits):
+                        v_interleave(s - 2)
+                    if 0 <= s - 1 < len(vunits):
+                        v_transpose(s - 1)
+                    if s < len(vunits):
+                        v_permute(s)
+                if tick >= 2 and (tick % 2 == 0 or tick >= nu):
+                    multiply(tick)

@@ -18,7 +18,7 @@ P = 128
 KP = 512
 NPASS = K // KP
 PERM_AHEAD = 3
-RAW_BUFS = 9
+RAW_BUFS = 8
 ACC_BANKS = 4
 
 ITEMS = (
@@ -27,8 +27,7 @@ ITEMS = (
     + [("X", 4), ("X", 5), ("V", 6), ("V", 7)]
 )
 GROUPS = [(m, 0) for m in range(4)] + [(m, 1) for m in range(4)] + [(m, h) for m in range(4, 8) for h in range(2)]
-V_FIRST_TICK = 20
-V_TICK_STEP = 3
+V_TICKS = (24, 26, 28, 30)
 
 
 def tile_tensoroutputlayer_kernel(tc, core, weights, out):
@@ -43,7 +42,7 @@ def tile_tensoroutputlayer_kernel(tc, core, weights, out):
         permp = ctx.enter_context(tc.tile_pool(name="permp", bufs=5))
         grpp = ctx.enter_context(tc.tile_pool(name="grpp", bufs=5))
         vecp = ctx.enter_context(tc.tile_pool(name="vecp", bufs=2))
-        outp = ctx.enter_context(tc.tile_pool(name="outp", bufs=4))
+        outp = ctx.enter_context(tc.tile_pool(name="outp", bufs=12))
         trp = ctx.enter_context(tc.psum_pool(name="trp", bufs=4))
         accp = ctx.enter_context(tc.psum_pool(name="accp", bufs=ACC_BANKS))
 
@@ -86,8 +85,8 @@ def tile_tensoroutputlayer_kernel(tc, core, weights, out):
                 nc.sync.dma_start(out=raw[:], in_=x2d[it[1] * P : (it[1] + 1) * P, :])
             else:
                 raw = rawp.tile([P, NPASS, 4, P], BF16, name="raw", tag="raw")
-                for a in range(4):
-                    for q in range(4):
+                for q in range(4):
+                    for a in (0, 2, 1, 3):
                         r0 = it[1] * P + 32 * q
                         nc.sync.dma_start(
                             out=raw[32 * a : 32 * a + 32, :, q, :],
@@ -233,15 +232,17 @@ def tile_tensoroutputlayer_kernel(tc, core, weights, out):
                     evacuate(tick + 1)
                 if 0 <= tick < nu:
                     quantize(units[tick][0:3], tick)
-                if tick >= V_FIRST_TICK and (tick - V_FIRST_TICK) % V_TICK_STEP == 0:
-                    s = (tick - V_FIRST_TICK) // V_TICK_STEP
-                    if 0 <= s - 3 < len(vunits):
-                        quantize(vunits[s - 3][0:3], tick)
-                    if 0 <= s - 2 < len(vunits):
-                        v_interleave(s - 2)
-                    if 0 <= s - 1 < len(vunits):
-                        v_transpose(s - 1)
-                    if s < len(vunits):
-                        v_permute(s)
+                for i, t0 in enumerate(V_TICKS):
+                    if tick == t0 + 3:
+                        quantize(vunits[i][0:3], tick)
+                for i, t0 in enumerate(V_TICKS):
+                    if tick == t0 + 2:
+                        v_interleave(i)
+                for i, t0 in enumerate(V_TICKS):
+                    if tick == t0 + 1:
+                        v_transpose(i)
+                for i, t0 in enumerate(V_TICKS):
+                    if tick == t0:
+                        v_permute(i)
                 if tick >= 2 and (tick % 2 == 0 or tick >= nu):
                     multiply(tick)

@@ -20,9 +20,12 @@ NPASS = K // KP
 PERM_AHEAD = 3
 RAW_BUFS = 8
 ACC_BANKS = 4
+Q_FIRST = True
+HEAD_TICKS = 8
+N_DIRECT = 0
 
 ITEMS = (
-    [("W", 0, 0), ("W", 0, 2), ("X", 0), ("X", 1), ("X", 2), ("X", 3), ("W", 0, 4), ("W", 0, 6)]
+    [("W", 0, 0), ("X", 0), ("X", 1), ("W", 0, 2), ("X", 2), ("X", 3), ("W", 0, 4), ("W", 0, 6)]
     + [("W", 1, c) for c in (0, 2, 4, 6)]
     + [("X", 4), ("X", 5), ("V", 6), ("V", 7)]
 )
@@ -64,7 +67,7 @@ def tile_tensoroutputlayer_kernel(tc, core, weights, out):
         nu = len(units)
 
         raw_tiles = {}
-        state = {"next_load": 0, "next_perm": 0, "open": 0, "stores": 0}
+        state = {"next_load": 0, "next_perm": 0, "open": 0, "stores": 0, "used": [], "freed": 0}
 
         def issue_load():
             i = state["next_load"]
@@ -100,9 +103,17 @@ def tile_tensoroutputlayer_kernel(tc, core, weights, out):
         codes = {}
         ready = {}
 
+        def consumed(item):
+            state["used"] = state["used"] + [item]
+            while state["freed"] in state["used"]:
+                state["freed"] = state["freed"] + 1
+                issue_load()
+
         def permute(j):
             kind, a0, b0, item, piece = units[j]
             raw = raw_tiles[item]
+            if j < N_DIRECT:
+                return
             perm = permp.tile([P, 4, 2, P], F32, name="perm", tag="perm")
             if kind == "W":
                 words = raw[:, :, piece * KP : (piece + 1) * KP].bitcast(F32)
@@ -113,18 +124,24 @@ def tile_tensoroutputlayer_kernel(tc, core, weights, out):
             nc.vector.tensor_copy(out=perm[:], in_=src)
             perm_tiles[j] = perm
             if piece == 1:
-                issue_load()
+                consumed(item)
 
         def transposes(j):
-            perm = perm_tiles[j]
+            kind, a0, b0, item, piece = units[j]
             banks = []
             for b in range(2):
                 bank = trp.tile([P, 2, 2, P], F32, name="trb", tag="trb")
                 for a in range(2):
                     for u in range(2):
-                        nc.tensor.transpose(bank[:, a, u, :], perm[:, 2 * b + a, u, :], ident[:])
+                        if j < N_DIRECT:
+                            words = raw_tiles[item][:, 2 * b + a, piece * KP : (piece + 1) * KP].bitcast(F32)
+                            nc.tensor.transpose(bank[:, a, u, :], words[:, u : 2 * P : 2], ident[:])
+                        else:
+                            nc.tensor.transpose(bank[:, a, u, :], perm_tiles[j][:, 2 * b + a, u, :], ident[:])
                 banks.append(bank)
             bank_tiles[j] = banks
+            if j < N_DIRECT and piece == 1:
+                consumed(item)
 
         def evacuate(j):
             grp = grpp.tile([P, 4 * P, 4], BF16, name="grp", tag="grp", align_bytes=64)
@@ -159,7 +176,7 @@ def tile_tensoroutputlayer_kernel(tc, core, weights, out):
             nc.scalar.copy(out=t[:], in_=words.rearrange("p (b j u) -> p b u j", j=32, u=2))
             vperm[i] = t
             if piece == 1:
-                issue_load()
+                consumed(item)
 
         def v_transpose(i):
             t = vecp.tile([P, 1024], F32, name="vturn", tag="vturn", align_bytes=64)
@@ -224,13 +241,15 @@ def tile_tensoroutputlayer_kernel(tc, core, weights, out):
             for i in range(RAW_BUFS):
                 issue_load()
             for tick in range(-PERM_AHEAD, nu + 12):
+                if Q_FIRST and 0 <= tick < nu:
+                    quantize(units[tick][0:3], tick)
                 for j in range(state["next_perm"], min(nu, tick + PERM_AHEAD + 1)):
                     permute(j)
                     state["next_perm"] = j + 1
                 if 0 <= tick + 1 < nu:
                     transposes(tick + 1)
                     evacuate(tick + 1)
-                if 0 <= tick < nu:
+                if (not Q_FIRST) and 0 <= tick < nu:
                     quantize(units[tick][0:3], tick)
                 for i, t0 in enumerate(V_TICKS):
                     if tick == t0 + 3:
@@ -244,5 +263,5 @@ def tile_tensoroutputlayer_kernel(tc, core, weights, out):
                 for i, t0 in enumerate(V_TICKS):
                     if tick == t0:
                         v_permute(i)
-                if tick >= 2 and (tick % 2 == 0 or tick >= nu):
+                if tick >= 2 and (tick % 2 == 0 or tick >= nu or tick <= HEAD_TICKS):
                     multiply(tick)

@@ -22,7 +22,7 @@ RAW_BUFS = 8
 ACC_BANKS = 4
 Q_FIRST = True
 HEAD_TICKS = 8
-N_DIRECT = 0
+N_DIRECT = 6
 
 ITEMS = (
     [("W", 0, 0), ("X", 0), ("X", 1), ("W", 0, 2), ("X", 2), ("X", 3), ("W", 0, 4), ("W", 0, 6)]
@@ -134,7 +134,11 @@ def tile_tensoroutputlayer_kernel(tc, core, weights, out):
                 for a in range(2):
                     for u in range(2):
                         if j < N_DIRECT:
-                            words = raw_tiles[item][:, 2 * b + a, piece * KP : (piece + 1) * KP].bitcast(F32)
+                            if kind == "W":
+                                words = raw_tiles[item][:, 2 * b + a, piece * KP : (piece + 1) * KP].bitcast(F32)
+                            else:
+                                k0 = (4 * piece + 2 * b + a) * KP
+                                words = raw_tiles[item][:, k0 : k0 + KP].bitcast(F32)
                             nc.tensor.transpose(bank[:, a, u, :], words[:, u : 2 * P : 2], ident[:])
                         else:
                             nc.tensor.transpose(bank[:, a, u, :], perm_tiles[j][:, 2 * b + a, u, :], ident[:])

from contextlib import ExitStack

import concourse.mybir as mybir
from concourse.masks import make_identity

ROWS = 1024
K = 4096
FLOPS = 2 * ROWS * ROWS * K

F32 = mybir.dt.float32
BF16 = mybir.dt.bfloat16
U32 = mybir.dt.uint32
U8 = mybir.dt.uint8
E5X4 = mybir.dt.float8_e5m2_x4
E4X4 = mybir.dt.float8_e4m3fn_x4

P = 128
KP = 512
NPASS = K // KP
PERM_AHEAD = 3
RAW_BUFS = 8
ACC_BANKS = 4
Q_FIRST = True
HEAD_TICKS = 8
N_DIRECT = 6

ITEMS = (
    [("W", 0, 0), ("X", 0), ("X", 1), ("W", 0, 2), ("X", 2), ("X", 3), ("W", 0, 4), ("W", 0, 6)]
    + [("W", 1, c) for c in (0, 2, 4, 6)]
    + [("X", 4), ("X", 5), ("V", 6), ("V", 7)]
)
GROUPS = [(m, 0) for m in range(4)] + [(m, 1) for m in range(4)] + [(m, h) for m in range(4, 8) for h in range(2)]
V_TICKS = (24, 26, 28, 30)


def tile_tensoroutputlayer_kernel(tc, core, weights, out):
    nc = tc.nc
    x2d = core.rearrange("b i j k -> b (i j k)")
    w2d = weights.rearrange("c i j k -> c (i j k)")

    with ExitStack() as ctx:
        const = ctx.enter_context(tc.tile_pool(name="const", bufs=1))
        keep = ctx.enter_context(tc.tile_pool(name="keep", bufs=1))
        rawp = ctx.enter_context(tc.tile_pool(name="rawp", bufs=RAW_BUFS))
        permp = ctx.enter_context(tc.tile_pool(name="permp", bufs=5))
        grpp = ctx.enter_context(tc.tile_pool(name="grpp", bufs=5))
        vecp = ctx.enter_context(tc.tile_pool(name="vecp", bufs=2))
        outp = ctx.enter_context(tc.tile_pool(name="outp", bufs=12))
        trp = ctx.enter_context(tc.psum_pool(name="trp", bufs=4))
        accp = ctx.enter_context(tc.psum_pool(name="accp", bufs=ACC_BANKS))

        ident = const.tile([P, P], F32, name="ident")
        make_identity(nc, ident[:])
        warm = const.tile([P, 8], F32, name="warm")
        nc.scalar.copy(out=warm[:, 0:1], in_=ident[:, 0:1])

        units = []
        vunits = []
        for i, it in enumerate(ITEMS):
            for piece in range(2):
                if it[0] == "W":
                    units.append(("W", it[1], it[2] + piece, i, piece))
                elif it[0] == "X":
                    units.append(("X", it[1], piece, i, piece))
                else:
                    vunits.append(("X", it[1], piece, i, piece))
        nu = len(units)

        raw_tiles = {}
        state = {"next_load": 0, "next_perm": 0, "open": 0, "stores": 0, "used": [], "freed": 0}

        def issue_load():
            i = state["next_load"]
            if i >= len(ITEMS):
                return
            state["next_load"] = i + 1
            it = ITEMS[i]
            if it[0] == "W":
                raw = rawp.tile([P, 4, 2 * KP], BF16, name="raw", tag="raw")
                r0 = it[1] * 512
                k0 = it[2] * KP
                nc.sync.dma_start(
                    out=raw[:],
                    in_=w2d[r0 : r0 + 512, k0 : k0 + 2 * KP].rearrange("(a p) k -> p a k", p=P),
                )
            elif it[0] == "X":
                raw = rawp.tile([P, K], BF16, name="raw", tag="raw")
                nc.sync.dma_start(out=raw[:], in_=x2d[it[1] * P : (it[1] + 1) * P, :])
            else:
                raw = rawp.tile([P, NPASS, 4, P], BF16, name="raw", tag="raw")
                for q in range(4):
                    for a in (0, 2, 1, 3):
                        r0 = it[1] * P + 32 * q
                        nc.sync.dma_start(
                            out=raw[32 * a : 32 * a + 32, :, q, :],
                            in_=x2d[r0 : r0 + 32, :].rearrange("i (c a k) -> i c a k", a=4, k=P)[:, :, a, :],
                        )
            raw_tiles[i] = raw

        perm_tiles = {}
        bank_tiles = {}
        grp_tiles = {}
        codes = {}
        ready = {}

        def consumed(item):
            state["used"] = state["used"] + [item]
            while state["freed"] in state["used"]:
                state["freed"] = state["freed"] + 1
                issue_load()

        def permute(j):
            kind, a0, b0, item, piece = units[j]
            raw = raw_tiles[item]
            if j < N_DIRECT:
                return
            perm = permp.tile([P, 4, 2, P], F32, name="perm", tag="perm")
            if kind == "W":
                words = raw[:, :, piece * KP : (piece + 1) * KP].bitcast(F32)
                src = words.rearrange("p a (q u) -> p a u q", u=2)
            else:
                words = raw[:, piece * 4 * KP : (piece + 1) * 4 * KP].bitcast(F32)
                src = words.rearrange("p (a q u) -> p a u q", a=4, u=2)
            nc.vector.tensor_copy(out=perm[:], in_=src)
            perm_tiles[j] = perm
            if piece == 1:
                consumed(item)

        def transposes(j):
            kind, a0, b0, item, piece = units[j]
            banks = []
            for b in range(2):
                bank = trp.tile([P, 2, 2, P], F32, name="trb", tag="trb")
                for a in range(2):
                    for u in range(2):
                        if j < N_DIRECT:
                            if kind == "W":
                                words = raw_tiles[item][:, 2 * b + a, piece * KP : (piece + 1) * KP].bitcast(F32)
                            else:
                                k0 = (4 * piece + 2 * b + a) * KP
                                words = raw_tiles[item][:, k0 : k0 + KP].bitcast(F32)
                            nc.tensor.transpose(bank[:, a, u, :], words[:, u : 2 * P : 2], ident[:])
                        else:
                            nc.tensor.transpose(bank[:, a, u, :], perm_tiles[j][:, 2 * b + a, u, :], ident[:])
                banks.append(bank)
            bank_tiles[j] = banks
            if j < N_DIRECT and piece == 1:
                consumed(item)

        def evacuate(j):
            grp = grpp.tile([P, 4 * P, 4], BF16, name="grp", tag="grp", align_bytes=64)
            gw = grp[:].bitcast(F32)
            for b in range(2):
                nc.scalar.copy(
                    out=gw[:, 2 * P * b : 2 * P * (b + 1), :].rearrange("p (a r) u -> p a r u", a=2),
                    in_=bank_tiles[j][b][:].rearrange("p a u r -> p a r u"),
                )
            grp_tiles[units[j][0:3]] = grp

        def quantize(key, tick):
            nm = "%s%d%d" % key
            cd = keep.tile([P, 4 * P], U32, name="cd" + nm, tag="cd" + nm, align_bytes=64)
            sc = keep.tile([P, 4 * P], U8, name="sc" + nm, tag="sc" + nm, align_bytes=64)
            nc.vector.quantize_mx(
                out=cd[:].bitcast(E5X4 if key[0] == "X" else E4X4),
                scales=sc[:],
                in_=grp_tiles[key][:].rearrange("p w t -> p (w t)"),
            )
            codes[key] = (cd, sc)
            ready[key] = tick

        vperm = {}
        vturn = {}

        def v_permute(i):
            kind, m, g, item, piece = vunits[i]
            raw = raw_tiles[item]
            t = vecp.tile([P, 16, 2, 32], F32, name="vperm", tag="vperm", align_bytes=64)
            words = raw[:, 4 * g : 4 * g + 4, :, :].rearrange("p c q k -> p (c q k)").bitcast(F32)
            nc.scalar.copy(out=t[:], in_=words.rearrange("p (b j u) -> p b u j", j=32, u=2))
            vperm[i] = t
            if piece == 1:
                consumed(item)

        def v_transpose(i):
            t = vecp.tile([P, 1024], F32, name="vturn", tag="vturn", align_bytes=64)
            nc.vector.transpose(out=t[:], in_=vperm[i][:].rearrange("p b u j -> p (b u j)"))
            vturn[i] = t

        def v_interleave(i):
            grp = grpp.tile([P, 4 * P, 4], BF16, name="grp", tag="grp", align_bytes=64)
            nc.vector.tensor_copy(
                out=grp[:].bitcast(F32).rearrange("p (b i) u -> p b i u", i=32),
                in_=vturn[i][:].rearrange("p (b u i) -> p b i u", u=2, i=32),
            )
            grp_tiles[vunits[i][0:3]] = grp

        def store(acc, m, h):
            n = state["stores"]
            state["stores"] = n + 1
            osb = outp.tile([P, 4 * P], F32, name="osb", tag="osb")
            nc.scalar.copy(out=osb[:], in_=acc[:])
            nc.sync.dma_start(out=out[m * P : (m + 1) * P, h * 512 : (h + 1) * 512], in_=osb[:])

        done = {}
        accs = {}

        def multiply(tick):
            for grp_key in GROUPS:
                m, h = grp_key
                d = done.setdefault(grp_key, [])
                if len(d) == NPASS:
                    continue
                avail = [
                    c
                    for c in range(NPASS)
                    if c not in d
                    and ready.get(("X", m, c // 4), tick) < tick
                    and ready.get(("W", h, c), tick) < tick
                ]
                if grp_key not in accs:
                    if len(avail) == 0 or state["open"] >= ACC_BANKS:
                        return
                    accs[grp_key] = accp.tile([P, 4 * P], F32, name="acc", tag="acc")
                    state["open"] = state["open"] + 1
                for c in avail:
                    xc, xs = codes[("X", m, c // 4)]
                    wc, ws = codes[("W", h, c)]
                    col = (c % 4) * P
                    nc.tensor.matmul_mx(
                        out=accs[grp_key][:],
                        lhsT=xc[:, col : col + P].bitcast(E5X4),
                        lhsT_scale=xs[:, col : col + P],
                        rhs=wc[:].bitcast(E4X4),
                        rhs_scale=ws[:],
                        start=(len(d) == 0),
                        stop=(len(d) == NPASS - 1),
                    )
                    d.append(c)
                if len(d) == NPASS:
                    store(accs[grp_key], m, h)
                    state["open"] = state["open"] - 1

        with tc.manual_schedule():
            for i in range(RAW_BUFS):
                issue_load()
            for tick in range(-PERM_AHEAD, nu + 12):
                if Q_FIRST and 0 <= tick < nu:
                    quantize(units[tick][0:3], tick)
                for j in range(state["next_perm"], min(nu, tick + PERM_AHEAD + 1)):
                    permute(j)
                    state["next_perm"] = j + 1
                if 0 <= tick + 1 < nu:
                    transposes(tick + 1)
                    evacuate(tick + 1)
                if (not Q_FIRST) and 0 <= tick < nu:
                    quantize(units[tick][0:3], tick)
                for i, t0 in enumerate(V_TICKS):
                    if tick == t0 + 3:
                        quantize(vunits[i][0:3], tick)
                for i, t0 in enumerate(V_TICKS):
                    if tick == t0 + 2:
                        v_interleave(i)
                for i, t0 in enumerate(V_TICKS):
                    if tick == t0 + 1:
                        v_transpose(i)
                for i, t0 in enumerate(V_TICKS):
                    if tick == t0:
                        v_permute(i)
                if tick >= 2 and (tick % 2 == 0 or tick >= nu or tick <= HEAD_TICKS):
                    multiply(tick)
